import numpy as np
import ml_dtypes


def mxq(x, axis, fmt="e4m3"):
    dtype, down = {"e4m3": (ml_dtypes.float8_e4m3fn, 7), "e5m2": (ml_dtypes.float8_e5m2, 14)}[fmt]
    v = np.moveaxis(np.asarray(x, np.float32).astype(ml_dtypes.bfloat16).astype(np.float64), axis, -1)
    blocks = v.reshape(v.shape[:-1] + (-1, 32))
    amax = np.abs(blocks).max(-1, keepdims=True)
    byte = np.maximum(np.where(amax > 0, np.frexp(amax)[1] - 1 + 127, 0) - down, 1)
    scale = np.exp2(byte - 127.0)
    codes = (blocks / scale).astype(np.float32).astype(dtype).astype(np.float64)
    return np.moveaxis((codes * scale).reshape(v.shape), -1, axis)


WIDE = False


def mx_kscale(k):
    if not WIDE:
        return np.ones(k)
    levels = np.array([10, -10, 5, -5, 0])
    a = np.random.permutation(np.resize(levels, k // 512 * 4)).reshape(k // 512, 4)
    idx = np.arange(k)
    return np.exp2(a[idx // 512, idx % 128 // 32])


BF16 = ml_dtypes.bfloat16


def bf(x):
    return np.asarray(x, np.float32).astype(BF16)


def f64(x):
    return np.asarray(x).astype(np.float64)


E2M1 = np.array([0.0, 0.5, 1.0, 1.5, 2.0, 3.0, 4.0, 6.0, -0.0, -0.5, -1.0, -1.5, -2.0, -3.0, -4.0, -6.0])


def pack_weight(w, fmt):
    k, n = w.shape
    w = f64(bf(w)).reshape(k // 32, 32, n)
    amax = np.abs(w).max(1)
    if fmt == "e4m3":
        byte = np.frexp(amax)[1] - 1 + 127 - 7
    else:
        mant, ex = np.frexp(amax / 6.0)
        byte = np.where(mant > 0.5, ex, ex - 1) + 127
    byte = np.clip(np.where(amax > 0, byte, 1), 1, 254)
    scaled = (w * np.exp2(127.0 - byte)[:, None, :]).reshape(k, n).astype(np.float32)
    by_word = np.ascontiguousarray(scaled.reshape(k // 512, 128, 4, n).transpose(0, 1, 3, 2))
    if fmt == "e4m3":
        words = by_word.astype(ml_dtypes.float8_e4m3fn).view(np.uint8)
    else:
        c = by_word.astype(ml_dtypes.float4_e2m1fn).view(np.uint8) & 0xF
        words = c[..., 0::2] | (c[..., 1::2] << 4)
    return np.ascontiguousarray(words), np.ascontiguousarray(byte.astype(np.uint8).reshape(k // 512, 16, n))


def unpack_weight(words, scales, fmt):
    g, p, n, _ = words.shape
    if fmt == "e4m3":
        vals = np.ascontiguousarray(words).view(ml_dtypes.float8_e4m3fn).astype(np.float64)
    else:
        nib = np.empty((g, p, n, 4), np.uint8)
        nib[..., 0::2] = words & 0xF
        nib[..., 1::2] = words >> 4
        vals = E2M1[nib]
    vals = vals * np.repeat(np.exp2(scales.astype(np.float64) - 127.0), 8, axis=1)[..., None]
    return vals.transpose(0, 1, 3, 2).reshape(g * 512, n)


B, C, H, W, F, KH, KW = 8, 512, 18, 16, 128, 3, 3
K = KH * KW * C
SPARSITY = 0.7
FMT = "e4m3"


def extract_patches(x, kh, kw):
    bb, s1, s2, cc = x.shape
    o1, o2 = s1 - kh + 1, s2 - kw + 1
    pats = np.stack([x[:, i:i + o1, j:j + o2, :] for i in range(kh) for j in range(kw)], axis=3)
    return pats.reshape(bb, o1, o2, kh * kw * cc)


def setup_inputs():
    s = mx_kscale(C)
    limit = np.sqrt(6.0 / (F + K))
    vals = np.random.uniform(-limit, limit, (F, K))
    mask = np.random.random((F, K)) >= SPARSITY
    mask[:, ::32] = True
    inputs = bf(np.random.standard_normal((B, C, H, W)) * s[None, :, None, None])
    kernel = vals * mask / np.tile(s, KH * KW)[None, :]
    words, scales = pack_weight(np.ascontiguousarray(kernel.T), FMT)
    return {"inputs": inputs, "kernel_words": words, "kernel_scales": scales}


def reference(inputs, kernel_words, kernel_scales):
    x = np.transpose(f64(inputs), (0, 3, 2, 1))
    p = extract_patches(x, KH, KW)
    p2 = np.ascontiguousarray(p.reshape(-1, K))
    wt = unpack_weight(kernel_words, kernel_scales, FMT)
    out = mxq(p2, 1, "e4m3") @ wt
    return out.reshape(p.shape[:3] + (F,)).transpose(0, 3, 1, 2)

@@ -1,0 +1,104 @@
+from contextlib import ExitStack
+
+import concourse.mybir as mybir
+
+BF16 = mybir.dt.bfloat16
+F32 = mybir.dt.float32
+I32 = mybir.dt.int32
+U8 = mybir.dt.uint8
+U32 = mybir.dt.uint32
+FP8X4 = mybir.dt.float8_e4m3fn_x4
+
+P = 128
+PACK = 4
+B, C, H, W, F = 8, 512, 18, 16, 128
+TAPS = 3
+OUT_D = H - TAPS + 1
+OUT_A = W - TAPS + 1
+
+GROUP = 4
+ROW = GROUP * W
+N_GROUPS = B // GROUP
+BANK = 512
+D_BANK = BANK // ROW
+QUANT_ROWS = 8
+VECTOR_ROWS = 12
+
+FLOPS = 2 * B * OUT_A * OUT_D * TAPS * TAPS * C * F
+
+
+def tile_sparseconv2d_kernel(tc, inputs, kernel_words, kernel_scales, out):
+    nc = tc.nc
+    with ExitStack() as ctx:
+        weights = ctx.enter_context(tc.tile_pool(name="weights", bufs=1))
+        images = ctx.enter_context(tc.tile_pool(name="images", bufs=B))
+        groups = ctx.enter_context(tc.tile_pool(name="groups", bufs=N_GROUPS))
+        psum = ctx.enter_context(tc.psum_pool(name="psum", bufs=8))
+
+        w_scales = weights.tile([P, TAPS * TAPS, F], U8, align_bytes=64)
+        nc.vector.memset(w_scales[:].bitcast(I32), 0)
+        scale_rows = kernel_scales.rearrange("g (q r) n -> r q g n", r=4)
+        for r in range(4):
+            nc.sync.dma_start(out=w_scales[r:P:32, :, :].bitcast(I32), in_=scale_rows[r].bitcast(I32))
+
+        def load_image(b):
+            x_raw = images.tile([P, PACK, H * W], BF16, name="x_raw")
+            nc.sync.dma_start(
+                out=x_raw[:].rearrange("p t n -> p (t n)"),
+                in_=inputs[b].rearrange("(p t) h w -> p (t h w)", t=PACK),
+            )
+            return x_raw
+
+        x_raws = [load_image(b) for b in range(GROUP)]
+
+        w_words = weights.tile([P, TAPS * TAPS, F], U32, align_bytes=64)
+        words = kernel_words.rearrange("g p n t -> p g (n t)").bitcast(I32)
+        for i in range(TAPS):
+            taps = slice(TAPS * i, TAPS * (i + 1))
+            nc.sync.dma_start(out=w_words[:, taps, :].bitcast(I32), in_=words[:, taps, :])
+
+        x_raws.extend(load_image(b) for b in range(GROUP, B))
+
+        for g in range(N_GROUPS):
+            grouped = groups.tile([P, H, GROUP, W, PACK], BF16, align_bytes=64)
+            for s in range(GROUP):
+                pixels = x_raws[GROUP * g + s][:].rearrange("p t (h w) -> p h w t", w=W)
+                nc.vector.tensor_copy(out=grouped[:, :VECTOR_ROWS, s, :, :], in_=pixels[:, :VECTOR_ROWS])
+                nc.scalar.copy(out=grouped[:, VECTOR_ROWS:, s, :, :], in_=pixels[:, VECTOR_ROWS:])
+
+            codes = groups.tile([P, H * ROW], U32, align_bytes=64)
+            scales = groups.tile([P, H * ROW], U8, align_bytes=64)
+            for h0 in range(0, H, QUANT_ROWS):
+                h1 = min(h0 + QUANT_ROWS, H)
+                nc.vector.quantize_mx(
+                    out=codes[:, h0 * ROW : h1 * ROW].bitcast(FP8X4),
+                    scales=scales[:, h0 * ROW : h1 * ROW],
+                    in_=grouped[:, h0:h1].rearrange("p h s w t -> p (h s w t)"),
+                )
+
+            result = groups.tile([P, GROUP, OUT_A, OUT_D], F32)
+            for d0 in range(0, OUT_D, D_BANK):
+                for i in range(TAPS):
+                    partial = psum.tile([P, BANK], F32)
+                    for j in range(TAPS):
+                        window = slice((d0 + j) * ROW, (d0 + j) * ROW + BANK)
+                        nc.tensor.matmul_mx(
+                            out=partial[:],
+                            lhsT=w_words[:, TAPS * i + j, :].bitcast(FP8X4),
+                            lhsT_scale=w_scales[:, TAPS * i + j, :],
+                            rhs=codes[:, window].bitcast(FP8X4),
+                            rhs_scale=scales[:, window],
+                            start=(j == 0),
+                            stop=(j == TAPS - 1),
+                        )
+                    shifted = partial[:].rearrange("p (d s w) -> p s w d", s=GROUP, w=W)[:, :, i : i + OUT_A, :]
+                    target = result[:, :, :, d0 : d0 + D_BANK]
+                    if i == 0:
+                        nc.scalar.copy(out=target, in_=shifted)
+                    else:
+                        nc.vector.tensor_add(out=target, in0=shifted, in1=target)
+
+            nc.sync.dma_start(
+                out=out[GROUP * g : GROUP * (g + 1)].rearrange("s f a d -> f s (a d)"),
+                in_=result[:].rearrange("p s a d -> p s (a d)"),
+            )

@@ -16,13 +16,11 @@ TAPS = 3
 OUT_D = H - TAPS + 1
 OUT_A = W - TAPS + 1
 
-GROUP = 4
-ROW = GROUP * W
-N_GROUPS = B // GROUP
-BANK = 512
-D_BANK = BANK // ROW
-QUANT_ROWS = 8
-VECTOR_ROWS = 12
+PAIR = 2
+ROW = PAIR * W
+N_PAIRS = B // PAIR
+BANK = OUT_D * ROW
+VECTOR_ROWS = 8
 
 FLOPS = 2 * B * OUT_A * OUT_D * TAPS * TAPS * C * F
 
@@ -30,16 +28,15 @@ FLOPS = 2 * B * OUT_A * OUT_D * TAPS * TAPS * C * F
 def tile_sparseconv2d_kernel(tc, inputs, kernel_words, kernel_scales, out):
     nc = tc.nc
     with ExitStack() as ctx:
-        weights = ctx.enter_context(tc.tile_pool(name="weights", bufs=1))
+        keep = ctx.enter_context(tc.tile_pool(name="keep", bufs=1))
         images = ctx.enter_context(tc.tile_pool(name="images", bufs=B))
-        groups = ctx.enter_context(tc.tile_pool(name="groups", bufs=N_GROUPS))
+        pairs = ctx.enter_context(tc.tile_pool(name="pairs", bufs=N_PAIRS))
         psum = ctx.enter_context(tc.psum_pool(name="psum", bufs=8))
 
-        w_scales = weights.tile([P, TAPS * TAPS, F], U8, align_bytes=64)
+        w_scales = keep.tile([P, TAPS * TAPS, F], U8, align_bytes=64)
+        x_scales = keep.tile([P, N_PAIRS, H * ROW], U8, align_bytes=64)
         nc.vector.memset(w_scales[:].bitcast(I32), 0)
-        scale_rows = kernel_scales.rearrange("g (q r) n -> r q g n", r=4)
-        for r in range(4):
-            nc.sync.dma_start(out=w_scales[r:P:32, :, :].bitcast(I32), in_=scale_rows[r].bitcast(I32))
+        nc.vector.memset(x_scales[:].bitcast(I32), 0)
 
         def load_image(b):
             x_raw = images.tile([P, PACK, H * W], BF16, name="x_raw")
@@ -49,56 +46,59 @@ def tile_sparseconv2d_kernel(tc, inputs, kernel_words, kernel_scales, out):
             )
             return x_raw
 
-        x_raws = [load_image(b) for b in range(GROUP)]
+        x_raws = [load_image(b) for b in range(PAIR)]
 
-        w_words = weights.tile([P, TAPS * TAPS, F], U32, align_bytes=64)
+        scale_rows = kernel_scales.rearrange("g (q r) n -> r q g n", r=4)
+        for r in range(4):
+            nc.sync.dma_start(out=w_scales[r:P:32, :, :].bitcast(I32), in_=scale_rows[r].bitcast(I32))
+
+        w_words = keep.tile([P, TAPS * TAPS, F], U32, align_bytes=64)
         words = kernel_words.rearrange("g p n t -> p g (n t)").bitcast(I32)
         for i in range(TAPS):
             taps = slice(TAPS * i, TAPS * (i + 1))
             nc.sync.dma_start(out=w_words[:, taps, :].bitcast(I32), in_=words[:, taps, :])
 
-        x_raws.extend(load_image(b) for b in range(GROUP, B))
+        x_raws.extend(load_image(b) for b in range(PAIR, B))
 
-        for g in range(N_GROUPS):
-            grouped = groups.tile([P, H, GROUP, W, PACK], BF16, align_bytes=64)
-            for s in range(GROUP):
-                pixels = x_raws[GROUP * g + s][:].rearrange("p t (h w) -> p h w t", w=W)
+        for g in range(N_PAIRS):
+            grouped = pairs.tile([P, H, PAIR, W, PACK], BF16, align_bytes=64)
+            for s in range(PAIR):
+                pixels = x_raws[PAIR * g + s][:].rearrange("p t (h w) -> p h w t", w=W)
                 nc.vector.tensor_copy(out=grouped[:, :VECTOR_ROWS, s, :, :], in_=pixels[:, :VECTOR_ROWS])
                 nc.scalar.copy(out=grouped[:, VECTOR_ROWS:, s, :, :], in_=pixels[:, VECTOR_ROWS:])
 
-            codes = groups.tile([P, H * ROW], U32, align_bytes=64)
-            scales = groups.tile([P, H * ROW], U8, align_bytes=64)
-            for h0 in range(0, H, QUANT_ROWS):
-                h1 = min(h0 + QUANT_ROWS, H)
+            codes = pairs.tile([P, H * ROW], U32, align_bytes=64)
+            scales = x_scales[:, g, :]
+            for h0, h1 in ((0, OUT_D), (OUT_D, H)):
                 nc.vector.quantize_mx(
                     out=codes[:, h0 * ROW : h1 * ROW].bitcast(FP8X4),
                     scales=scales[:, h0 * ROW : h1 * ROW],
                     in_=grouped[:, h0:h1].rearrange("p h s w t -> p (h s w t)"),
                 )
+            scales_from_row_1 = pairs.tile([P, BANK], U8, align_bytes=64)
+            nc.vector.tensor_copy(out=scales_from_row_1[:].bitcast(I32), in_=scales[:, ROW : ROW + BANK].bitcast(I32))
+            window_scales = [scales[:, 0:BANK], scales_from_row_1[:], scales[:, 2 * ROW : 2 * ROW + BANK]]
 
-            result = groups.tile([P, GROUP, OUT_A, OUT_D], F32)
-            for d0 in range(0, OUT_D, D_BANK):
-                for i in range(TAPS):
-                    partial = psum.tile([P, BANK], F32)
-                    for j in range(TAPS):
-                        window = slice((d0 + j) * ROW, (d0 + j) * ROW + BANK)
-                        nc.tensor.matmul_mx(
-                            out=partial[:],
-                            lhsT=w_words[:, TAPS * i + j, :].bitcast(FP8X4),
-                            lhsT_scale=w_scales[:, TAPS * i + j, :],
-                            rhs=codes[:, window].bitcast(FP8X4),
-                            rhs_scale=scales[:, window],
-                            start=(j == 0),
-                            stop=(j == TAPS - 1),
-                        )
-                    shifted = partial[:].rearrange("p (d s w) -> p s w d", s=GROUP, w=W)[:, :, i : i + OUT_A, :]
-                    target = result[:, :, :, d0 : d0 + D_BANK]
-                    if i == 0:
-                        nc.scalar.copy(out=target, in_=shifted)
-                    else:
-                        nc.vector.tensor_add(out=target, in0=shifted, in1=target)
+            result = pairs.tile([P, PAIR, OUT_A, OUT_D], F32)
+            for i in range(TAPS):
+                partial = psum.tile([P, BANK], F32)
+                for j in range(TAPS):
+                    nc.tensor.matmul_mx(
+                        out=partial[:],
+                        lhsT=w_words[:, TAPS * i + j, :].bitcast(FP8X4),
+                        lhsT_scale=w_scales[:, TAPS * i + j, :],
+                        rhs=codes[:, j * ROW : j * ROW + BANK].bitcast(FP8X4),
+                        rhs_scale=window_scales[j],
+                        start=(j == 0),
+                        stop=(j == TAPS - 1),
+                    )
+                shifted = partial[:].rearrange("p (d s w) -> p s w d", s=PAIR, w=W)[:, :, i : i + OUT_A, :]
+                if i == 0:
+                    nc.scalar.copy(out=result[:], in_=shifted)
+                else:
+                    nc.vector.tensor_add(out=result[:], in0=shifted, in1=result[:])
 
             nc.sync.dma_start(
-                out=out[GROUP * g : GROUP * (g + 1)].rearrange("s f a d -> f s (a d)"),
+                out=out[PAIR * g : PAIR * (g + 1)].rearrange("s f a d -> f s (a d)"),
                 in_=result[:].rearrange("p s a d -> p s (a d)"),
             )

@@ -20,6 +20,7 @@ PAIR = 2
 ROW = PAIR * W
 N_PAIRS = B // PAIR
 BANK = OUT_D * ROW
+AHEAD = 2
 VECTOR_ROWS = 8
 
 FLOPS = 2 * B * OUT_A * OUT_D * TAPS * TAPS * C * F
@@ -60,14 +61,14 @@ def tile_sparseconv2d_kernel(tc, inputs, kernel_words, kernel_scales, out):
 
         x_raws.extend(load_image(b) for b in range(PAIR, B))
 
-        for g in range(N_PAIRS):
-            grouped = pairs.tile([P, H, PAIR, W, PACK], BF16, align_bytes=64)
+        def quantise_pair(g):
+            grouped = pairs.tile([P, H, PAIR, W, PACK], BF16, align_bytes=64, name="grouped")
             for s in range(PAIR):
                 pixels = x_raws[PAIR * g + s][:].rearrange("p t (h w) -> p h w t", w=W)
                 nc.vector.tensor_copy(out=grouped[:, :VECTOR_ROWS, s, :, :], in_=pixels[:, :VECTOR_ROWS])
                 nc.scalar.copy(out=grouped[:, VECTOR_ROWS:, s, :, :], in_=pixels[:, VECTOR_ROWS:])
 
-            codes = pairs.tile([P, H * ROW], U32, align_bytes=64)
+            codes = pairs.tile([P, H * ROW], U32, align_bytes=64, name="codes")
             scales = x_scales[:, g, :]
             for h0, h1 in ((0, OUT_D), (OUT_D, H)):
                 nc.vector.quantize_mx(
@@ -75,13 +76,14 @@ def tile_sparseconv2d_kernel(tc, inputs, kernel_words, kernel_scales, out):
                     scales=scales[:, h0 * ROW : h1 * ROW],
                     in_=grouped[:, h0:h1].rearrange("p h s w t -> p (h s w t)"),
                 )
-            scales_from_row_1 = pairs.tile([P, BANK], U8, align_bytes=64)
+            scales_from_row_1 = pairs.tile([P, BANK], U8, align_bytes=64, name="scales_from_row_1")
             nc.vector.tensor_copy(out=scales_from_row_1[:].bitcast(I32), in_=scales[:, ROW : ROW + BANK].bitcast(I32))
-            window_scales = [scales[:, 0:BANK], scales_from_row_1[:], scales[:, 2 * ROW : 2 * ROW + BANK]]
+            return codes, [scales[:, 0:BANK], scales_from_row_1[:], scales[:, 2 * ROW : 2 * ROW + BANK]]
 
-            result = pairs.tile([P, PAIR, OUT_A, OUT_D], F32)
+        def convolve_pair(g, codes, window_scales):
+            result = pairs.tile([P, PAIR, OUT_A, OUT_D], F32, name="result")
             for i in range(TAPS):
-                partial = psum.tile([P, BANK], F32)
+                partial = psum.tile([P, BANK], F32, name="partial")
                 for j in range(TAPS):
                     nc.tensor.matmul_mx(
                         out=partial[:],
@@ -102,3 +104,12 @@ def tile_sparseconv2d_kernel(tc, inputs, kernel_words, kernel_scales, out):
                 out=out[PAIR * g : PAIR * (g + 1)].rearrange("s f a d -> f s (a d)"),
                 in_=result[:].rearrange("p s a d -> p s (a d)"),
             )
+
+        with tc.manual_schedule():
+            quantised = []
+            for step in range(N_PAIRS + AHEAD):
+                if step < N_PAIRS:
+                    quantised.append(quantise_pair(step))
+                if step >= AHEAD:
+                    codes, window_scales = quantised[step - AHEAD]
+                    convolve_pair(step - AHEAD, codes, window_scales)

@@ -20,8 +20,9 @@ PAIR = 2
 ROW = PAIR * W
 N_PAIRS = B // PAIR
 BANK = OUT_D * ROW
+WARM_UP = 10
 AHEAD = 2
-VECTOR_ROWS = 8
+SCALAR_ROWS = 10
 
 FLOPS = 2 * B * OUT_A * OUT_D * TAPS * TAPS * C * F
 
@@ -33,6 +34,12 @@ def tile_sparseconv2d_kernel(tc, inputs, kernel_words, kernel_scales, out):
         images = ctx.enter_context(tc.tile_pool(name="images", bufs=B))
         pairs = ctx.enter_context(tc.tile_pool(name="pairs", bufs=N_PAIRS))
         psum = ctx.enter_context(tc.psum_pool(name="psum", bufs=8))
+
+        zeros = keep.tile([P, BANK], BF16)
+        nc.vector.memset(zeros[:], 0.0)
+        unread = psum.tile([P, BANK], F32, name="partial")
+        for warm in range(WARM_UP):
+            nc.tensor.matmul(out=unread[:], lhsT=zeros[:, :P], rhs=zeros[:], start=True, stop=True)
 
         w_scales = keep.tile([P, TAPS * TAPS, F], U8, align_bytes=64)
         x_scales = keep.tile([P, N_PAIRS, H * ROW], U8, align_bytes=64)
@@ -47,26 +54,36 @@ def tile_sparseconv2d_kernel(tc, inputs, kernel_words, kernel_scales, out):
             )
             return x_raw
 
-        x_raws = [load_image(b) for b in range(PAIR)]
-
-        scale_rows = kernel_scales.rearrange("g (q r) n -> r q g n", r=4)
-        for r in range(4):
-            nc.sync.dma_start(out=w_scales[r:P:32, :, :].bitcast(I32), in_=scale_rows[r].bitcast(I32))
-
         w_words = keep.tile([P, TAPS * TAPS, F], U32, align_bytes=64)
         words = kernel_words.rearrange("g p n t -> p g (n t)").bitcast(I32)
-        for i in range(TAPS):
+
+        def load_weights(i):
             taps = slice(TAPS * i, TAPS * (i + 1))
             nc.sync.dma_start(out=w_words[:, taps, :].bitcast(I32), in_=words[:, taps, :])
 
-        x_raws.extend(load_image(b) for b in range(PAIR, B))
+        x_raws = [load_image(b) for b in range(PAIR)]
+        scale_rows = kernel_scales.rearrange("g (q r) n -> r q g n", r=4)
+        for r in range(4):
+            nc.sync.dma_start(out=w_scales[r:P:32, :, :].bitcast(I32), in_=scale_rows[r].bitcast(I32))
+        load_weights(0)
+        load_weights(1)
+        x_raws.extend(load_image(b) for b in range(PAIR, 2 * PAIR))
+        load_weights(2)
+        x_raws.extend(load_image(b) for b in range(2 * PAIR, B))
 
         def quantise_pair(g):
             grouped = pairs.tile([P, H, PAIR, W, PACK], BF16, align_bytes=64, name="grouped")
             for s in range(PAIR):
                 pixels = x_raws[PAIR * g + s][:].rearrange("p t (h w) -> p h w t", w=W)
-                nc.vector.tensor_copy(out=grouped[:, :VECTOR_ROWS, s, :, :], in_=pixels[:, :VECTOR_ROWS])
-                nc.scalar.copy(out=grouped[:, VECTOR_ROWS:, s, :, :], in_=pixels[:, VECTOR_ROWS:])
+                nc.scalar.copy(out=grouped[:, :SCALAR_ROWS, s, :, :], in_=pixels[:, :SCALAR_ROWS])
+                nc.gpsimd.tensor_scalar(
+                    out=grouped[:, SCALAR_ROWS:, s, :, :],
+                    in0=pixels[:, SCALAR_ROWS:],
+                    scalar1=1.0,
+                    scalar2=0.0,
+                    op0=mybir.AluOpType.mult,
+                    op1=mybir.AluOpType.add,
+                )
 
             codes = pairs.tile([P, H * ROW], U32, align_bytes=64, name="codes")
             scales = x_scales[:, g, :]

@@ -13,6 +13,7 @@ P = 128
 PACK = 4
 B, C, H, W, F = 8, 512, 18, 16, 128
 TAPS = 3
+ROW_TAPS = (0, 2, 1)
 OUT_D = H - TAPS + 1
 OUT_A = W - TAPS + 1
 
@@ -22,7 +23,7 @@ N_PAIRS = B // PAIR
 BANK = OUT_D * ROW
 WARM_UP = 10
 AHEAD = 2
-SCALAR_ROWS = 10
+VECTOR_ROWS = 8
 
 FLOPS = 2 * B * OUT_A * OUT_D * TAPS * TAPS * C * F
 
@@ -71,62 +72,65 @@ def tile_sparseconv2d_kernel(tc, inputs, kernel_words, kernel_scales, out):
         load_weights(2)
         x_raws.extend(load_image(b) for b in range(2 * PAIR, B))
 
-        def quantise_pair(g):
+        def regroup(g):
             grouped = pairs.tile([P, H, PAIR, W, PACK], BF16, align_bytes=64, name="grouped")
             for s in range(PAIR):
                 pixels = x_raws[PAIR * g + s][:].rearrange("p t (h w) -> p h w t", w=W)
-                nc.scalar.copy(out=grouped[:, :SCALAR_ROWS, s, :, :], in_=pixels[:, :SCALAR_ROWS])
-                nc.gpsimd.tensor_scalar(
-                    out=grouped[:, SCALAR_ROWS:, s, :, :],
-                    in0=pixels[:, SCALAR_ROWS:],
-                    scalar1=1.0,
-                    scalar2=0.0,
-                    op0=mybir.AluOpType.mult,
-                    op1=mybir.AluOpType.add,
-                )
+                nc.vector.tensor_copy(out=grouped[:, :VECTOR_ROWS, s, :, :], in_=pixels[:, :VECTOR_ROWS])
+                nc.scalar.copy(out=grouped[:, VECTOR_ROWS:, s, :, :], in_=pixels[:, VECTOR_ROWS:])
+            return grouped
 
+        def quantise(g, grouped):
             codes = pairs.tile([P, H * ROW], U32, align_bytes=64, name="codes")
-            scales = x_scales[:, g, :]
             for h0, h1 in ((0, OUT_D), (OUT_D, H)):
                 nc.vector.quantize_mx(
                     out=codes[:, h0 * ROW : h1 * ROW].bitcast(FP8X4),
-                    scales=scales[:, h0 * ROW : h1 * ROW],
+                    scales=x_scales[:, g, h0 * ROW : h1 * ROW],
                     in_=grouped[:, h0:h1].rearrange("p h s w t -> p (h s w t)"),
                 )
-            scales_from_row_1 = pairs.tile([P, BANK], U8, align_bytes=64, name="scales_from_row_1")
-            nc.vector.tensor_copy(out=scales_from_row_1[:].bitcast(I32), in_=scales[:, ROW : ROW + BANK].bitcast(I32))
-            return codes, [scales[:, 0:BANK], scales_from_row_1[:], scales[:, 2 * ROW : 2 * ROW + BANK]]
+            return codes
 
-        def convolve_pair(g, codes, window_scales):
-            result = pairs.tile([P, PAIR, OUT_A, OUT_D], F32, name="result")
-            for i in range(TAPS):
-                partial = psum.tile([P, BANK], F32, name="partial")
-                for j in range(TAPS):
-                    nc.tensor.matmul_mx(
-                        out=partial[:],
-                        lhsT=w_words[:, TAPS * i + j, :].bitcast(FP8X4),
-                        lhsT_scale=w_scales[:, TAPS * i + j, :],
-                        rhs=codes[:, j * ROW : j * ROW + BANK].bitcast(FP8X4),
-                        rhs_scale=window_scales[j],
-                        start=(j == 0),
-                        stop=(j == TAPS - 1),
-                    )
-                shifted = partial[:].rearrange("p (d s w) -> p s w d", s=PAIR, w=W)[:, :, i : i + OUT_A, :]
-                if i == 0:
-                    nc.scalar.copy(out=result[:], in_=shifted)
-                else:
-                    nc.vector.tensor_add(out=result[:], in0=shifted, in1=result[:])
+        def shift_scales(g):
+            from_row_1 = pairs.tile([P, BANK], U8, align_bytes=64, name="from_row_1")
+            nc.vector.tensor_copy(out=from_row_1[:].bitcast(I32), in_=x_scales[:, g, ROW : ROW + BANK].bitcast(I32))
+            return [x_scales[:, g, 0:BANK], from_row_1[:], x_scales[:, g, 2 * ROW : 2 * ROW + BANK]]
 
-            nc.sync.dma_start(
-                out=out[PAIR * g : PAIR * (g + 1)].rearrange("s f a d -> f s (a d)"),
-                in_=result[:].rearrange("p s a d -> p s (a d)"),
-            )
+        def multiply(i, codes, window_scales):
+            partial = psum.tile([P, BANK], F32, name="partial")
+            for j in ROW_TAPS:
+                nc.tensor.matmul_mx(
+                    out=partial[:],
+                    lhsT=w_words[:, TAPS * i + j, :].bitcast(FP8X4),
+                    lhsT_scale=w_scales[:, TAPS * i + j, :],
+                    rhs=codes[:, j * ROW : j * ROW + BANK].bitcast(FP8X4),
+                    rhs_scale=window_scales[j],
+                    start=(j == ROW_TAPS[0]),
+                    stop=(j == ROW_TAPS[-1]),
+                )
+            return partial[:].rearrange("p (d s w) -> p s w d", s=PAIR, w=W)[:, :, i : i + OUT_A, :]
 
         with tc.manual_schedule():
-            quantised = []
+            operands = []
             for step in range(N_PAIRS + AHEAD):
-                if step < N_PAIRS:
-                    quantised.append(quantise_pair(step))
-                if step >= AHEAD:
-                    codes, window_scales = quantised[step - AHEAD]
-                    convolve_pair(step - AHEAD, codes, window_scales)
+                feeds = step < N_PAIRS
+                sums = step >= AHEAD
+                g = step - AHEAD
+                if feeds:
+                    grouped = regroup(step)
+                if sums:
+                    codes, window_scales = operands[g]
+                    shifted = [multiply(i, codes, window_scales) for i in range(TAPS)]
+                    result = pairs.tile([P, PAIR, OUT_A, OUT_D], F32, name="result")
+                    nc.scalar.copy(out=result[:], in_=shifted[0])
+                    nc.vector.tensor_add(out=result[:], in0=shifted[1], in1=result[:])
+                if feeds:
+                    new_codes = quantise(step, grouped)
+                if sums:
+                    nc.vector.tensor_add(out=result[:], in0=shifted[2], in1=result[:])
+                if feeds:
+                    operands.append((new_codes, shift_scales(step)))
+                if sums:
+                    nc.sync.dma_start(
+                        out=out[PAIR * g : PAIR * (g + 1)].rearrange("s f a d -> f s (a d)"),
+                        in_=result[:].rearrange("p s a d -> p s (a d)"),
+                    )

@@ -21,9 +21,10 @@ PAIR = 2
 ROW = PAIR * W
 N_PAIRS = B // PAIR
 BANK = OUT_D * ROW
-WARM_UP = 10
+WARM_UP = 8
 AHEAD = 2
-VECTOR_ROWS = 8
+VECTOR_ROWS_AT_FIRST = 12
+VECTOR_ROWS_BESIDE_SUMS = 8
 
 FLOPS = 2 * B * OUT_A * OUT_D * TAPS * TAPS * C * F
 
@@ -72,12 +73,12 @@ def tile_sparseconv2d_kernel(tc, inputs, kernel_words, kernel_scales, out):
         load_weights(2)
         x_raws.extend(load_image(b) for b in range(2 * PAIR, B))
 
-        def regroup(g):
+        def regroup(g, vector_rows):
             grouped = pairs.tile([P, H, PAIR, W, PACK], BF16, align_bytes=64, name="grouped")
             for s in range(PAIR):
                 pixels = x_raws[PAIR * g + s][:].rearrange("p t (h w) -> p h w t", w=W)
-                nc.vector.tensor_copy(out=grouped[:, :VECTOR_ROWS, s, :, :], in_=pixels[:, :VECTOR_ROWS])
-                nc.scalar.copy(out=grouped[:, VECTOR_ROWS:, s, :, :], in_=pixels[:, VECTOR_ROWS:])
+                nc.vector.tensor_copy(out=grouped[:, :vector_rows, s, :, :], in_=pixels[:, :vector_rows])
+                nc.scalar.copy(out=grouped[:, vector_rows:, s, :, :], in_=pixels[:, vector_rows:])
             return grouped
 
         def quantise(g, grouped):
@@ -115,13 +116,14 @@ def tile_sparseconv2d_kernel(tc, inputs, kernel_words, kernel_scales, out):
                 feeds = step < N_PAIRS
                 sums = step >= AHEAD
                 g = step - AHEAD
-                if feeds:
-                    grouped = regroup(step)
                 if sums:
                     codes, window_scales = operands[g]
                     shifted = [multiply(i, codes, window_scales) for i in range(TAPS)]
                     result = pairs.tile([P, PAIR, OUT_A, OUT_D], F32, name="result")
                     nc.scalar.copy(out=result[:], in_=shifted[0])
+                if feeds:
+                    grouped = regroup(step, VECTOR_ROWS_BESIDE_SUMS if sums else VECTOR_ROWS_AT_FIRST)
+                if sums:
                     nc.vector.tensor_add(out=result[:], in0=shifted[1], in1=result[:])
                 if feeds:
                     new_codes = quantise(step, grouped)

@@ -21,6 +21,8 @@ PAIR = 2
 ROW = PAIR * W
 N_PAIRS = B // PAIR
 BANK = OUT_D * ROW
+IMAGE = H * W
+HALF = OUT_D * W
 WARM_UP = 8
 AHEAD = 2
 VECTOR_ROWS_AT_FIRST = 12
@@ -74,11 +76,13 @@ def tile_sparseconv2d_kernel(tc, inputs, kernel_words, kernel_scales, out):
         x_raws.extend(load_image(b) for b in range(2 * PAIR, B))
 
         def regroup(g, vector_rows):
-            grouped = pairs.tile([P, H, PAIR, W, PACK], BF16, align_bytes=64, name="grouped")
+            grouped = pairs.tile([P, H * PAIR * W * PACK], BF16, align_bytes=64, name="grouped")
+            order = "p (s h w t) -> p h s w t" if g == N_PAIRS - 1 else "p (h s w t) -> p h s w t"
+            places = grouped[:].rearrange(order, s=PAIR, w=W, t=PACK)
             for s in range(PAIR):
                 pixels = x_raws[PAIR * g + s][:].rearrange("p t (h w) -> p h w t", w=W)
-                nc.vector.tensor_copy(out=grouped[:, :vector_rows, s, :, :], in_=pixels[:, :vector_rows])
-                nc.scalar.copy(out=grouped[:, vector_rows:, s, :, :], in_=pixels[:, vector_rows:])
+                nc.vector.tensor_copy(out=places[:, :vector_rows, s, :, :], in_=pixels[:, :vector_rows])
+                nc.scalar.copy(out=places[:, vector_rows:, s, :, :], in_=pixels[:, vector_rows:])
             return grouped
 
         def quantise(g, grouped):
@@ -87,7 +91,7 @@ def tile_sparseconv2d_kernel(tc, inputs, kernel_words, kernel_scales, out):
                 nc.vector.quantize_mx(
                     out=codes[:, h0 * ROW : h1 * ROW].bitcast(FP8X4),
                     scales=x_scales[:, g, h0 * ROW : h1 * ROW],
-                    in_=grouped[:, h0:h1].rearrange("p h s w t -> p (h s w t)"),
+                    in_=grouped[:, h0 * ROW * PACK : h1 * ROW * PACK],
                 )
             return codes
 
@@ -110,12 +114,50 @@ def tile_sparseconv2d_kernel(tc, inputs, kernel_words, kernel_scales, out):
                 )
             return partial[:].rearrange("p (d s w) -> p s w d", s=PAIR, w=W)[:, :, i : i + OUT_A, :]
 
+        def shift_scales_of_images(g):
+            moved = pairs.tile([P, TAPS, BANK], U8, align_bytes=64, name="moved")
+            windows = {(0, 0): x_scales[:, g, 0:HALF], (1, 2): x_scales[:, g, IMAGE + 2 * W : IMAGE + 2 * W + HALF]}
+            for k, (first, images_served) in enumerate(((2 * W, ((0, 2), (1, 0))), (W, ((0, 1),)), (IMAGE + W, ((1, 1),)))):
+                width = HALF * len(images_served)
+                nc.vector.tensor_copy(
+                    out=moved[:, k, :width].bitcast(I32), in_=x_scales[:, g, first : first + width].bitcast(I32)
+                )
+                for n, key in enumerate(images_served):
+                    windows[key] = moved[:, k, n * HALF : (n + 1) * HALF]
+            return windows
+
+        def multiply_image(i, s, codes, windows):
+            partial = psum.tile([P, HALF], F32, name="partial")
+            for j in ROW_TAPS:
+                first = IMAGE * s + W * j
+                nc.tensor.matmul_mx(
+                    out=partial[:],
+                    lhsT=w_words[:, TAPS * i + j, :].bitcast(FP8X4),
+                    lhsT_scale=w_scales[:, TAPS * i + j, :],
+                    rhs=codes[:, first : first + HALF].bitcast(FP8X4),
+                    rhs_scale=windows[(s, j)],
+                    start=(j == ROW_TAPS[0]),
+                    stop=(j == ROW_TAPS[-1]),
+                )
+            return partial[:].rearrange("p (d w) -> p w d", w=W)[:, i : i + OUT_A, :]
+
         with tc.manual_schedule():
             operands = []
             for step in range(N_PAIRS + AHEAD):
                 feeds = step < N_PAIRS
-                sums = step >= AHEAD
                 g = step - AHEAD
+                sums = 0 <= g < N_PAIRS - 1
+                if g == N_PAIRS - 1:
+                    codes, window_scales = operands[g]
+                    for s in range(PAIR):
+                        shifted = [multiply_image(i, s, codes, window_scales) for i in range(TAPS)]
+                        result = pairs.tile([P, OUT_A, OUT_D], F32, name="result_of_image")
+                        nc.scalar.copy(out=result[:], in_=shifted[0])
+                        nc.vector.tensor_add(out=result[:], in0=shifted[1], in1=result[:])
+                        nc.vector.tensor_add(out=result[:], in0=shifted[2], in1=result[:])
+                        nc.sync.dma_start(
+                            out=out[PAIR * g + s].rearrange("f a d -> f (a d)"), in_=result[:].rearrange("p a d -> p (a d)")
+                        )
                 if sums:
                     codes, window_scales = operands[g]
                     shifted = [multiply(i, codes, window_scales) for i in range(TAPS)]
@@ -130,7 +172,9 @@ def tile_sparseconv2d_kernel(tc, inputs, kernel_words, kernel_scales, out):
                 if sums:
                     nc.vector.tensor_add(out=result[:], in0=shifted[2], in1=result[:])
                 if feeds:
-                    operands.append((new_codes, shift_scales(step)))
+                    operands.append(
+                        (new_codes, shift_scales_of_images(step) if step == N_PAIRS - 1 else shift_scales(step))
+                    )
                 if sums:
                     nc.sync.dma_start(
                         out=out[PAIR * g : PAIR * (g + 1)].rearrange("s f a d -> f s (a d)"),

@@ -149,12 +149,18 @@ def tile_sparseconv2d_kernel(tc, inputs, kernel_words, kernel_scales, out):
                 sums = 0 <= g < N_PAIRS - 1
                 if g == N_PAIRS - 1:
                     codes, window_scales = operands[g]
+                    results = []
                     for s in range(PAIR):
-                        shifted = [multiply_image(i, s, codes, window_scales) for i in range(TAPS)]
+                        shifted = [multiply_image(i, s, codes, window_scales) for i in range(TAPS - 1)]
                         result = pairs.tile([P, OUT_A, OUT_D], F32, name="result_of_image")
                         nc.scalar.copy(out=result[:], in_=shifted[0])
                         nc.vector.tensor_add(out=result[:], in0=shifted[1], in1=result[:])
-                        nc.vector.tensor_add(out=result[:], in0=shifted[2], in1=result[:])
+                        results.append(result)
+                    for s in range(PAIR):
+                        result = results[s]
+                        nc.vector.tensor_add(
+                            out=result[:], in0=multiply_image(TAPS - 1, s, codes, window_scales), in1=result[:]
+                        )
                         nc.sync.dma_start(
                             out=out[PAIR * g + s].rearrange("f a d -> f (a d)"), in_=result[:].rearrange("p a d -> p (a d)")
                         )

@@ -126,16 +126,16 @@ def tile_sparseconv2d_kernel(tc, inputs, kernel_words, kernel_scales, out):
                     windows[key] = moved[:, k, n * HALF : (n + 1) * HALF]
             return windows
 
-        def multiply_image(i, s, codes, windows):
-            partial = psum.tile([P, HALF], F32, name="partial")
+        def multiply_image(i, s, codes, windows, d0=0, d1=OUT_D):
+            partial = psum.tile([P, (d1 - d0) * W], F32, name="partial")
             for j in ROW_TAPS:
                 first = IMAGE * s + W * j
                 nc.tensor.matmul_mx(
                     out=partial[:],
                     lhsT=w_words[:, TAPS * i + j, :].bitcast(FP8X4),
                     lhsT_scale=w_scales[:, TAPS * i + j, :],
-                    rhs=codes[:, first : first + HALF].bitcast(FP8X4),
-                    rhs_scale=windows[(s, j)],
+                    rhs=codes[:, first + d0 * W : first + d1 * W].bitcast(FP8X4),
+                    rhs_scale=windows[(s, j)][:, d0 * W : d1 * W],
                     start=(j == ROW_TAPS[0]),
                     stop=(j == ROW_TAPS[-1]),
                 )
@@ -158,9 +158,12 @@ def tile_sparseconv2d_kernel(tc, inputs, kernel_words, kernel_scales, out):
                         results.append(result)
                     for s in range(PAIR):
                         result = results[s]
-                        nc.vector.tensor_add(
-                            out=result[:], in0=multiply_image(TAPS - 1, s, codes, window_scales), in1=result[:]
-                        )
+                        for d0, d1 in ((0, OUT_D),) if s == 0 else ((0, OUT_D // 2), (OUT_D // 2, OUT_D)):
+                            nc.vector.tensor_add(
+                                out=result[:, :, d0:d1],
+                                in0=multiply_image(TAPS - 1, s, codes, window_scales, d0, d1),
+                                in1=result[:, :, d0:d1],
+                            )
                         nc.sync.dma_start(
                             out=out[PAIR * g + s].rearrange("f a d -> f (a d)"), in_=result[:].rearrange("p a d -> p (a d)")
                         )

@@ -19,14 +19,14 @@ OUT_A = W - TAPS + 1
 
 PAIR = 2
 ROW = PAIR * W
-N_PAIRS = B // PAIR
 BANK = OUT_D * ROW
 IMAGE = H * W
 HALF = OUT_D * W
-WARM_UP = 8
-AHEAD = 2
-VECTOR_ROWS_AT_FIRST = 12
-VECTOR_ROWS_BESIDE_SUMS = 8
+PLANE = 320
+SINGLES = (0, 1, 2, 3, 6, 7)
+JOINT = (4, 5)
+WARM_UP = 6
+VECTOR_ROWS = (12, 12, 10, 10, 8, 8, 6, 6)
 
 FLOPS = 2 * B * OUT_A * OUT_D * TAPS * TAPS * C * F
 
@@ -36,7 +36,6 @@ def tile_sparseconv2d_kernel(tc, inputs, kernel_words, kernel_scales, out):
     with ExitStack() as ctx:
         keep = ctx.enter_context(tc.tile_pool(name="keep", bufs=1))
         images = ctx.enter_context(tc.tile_pool(name="images", bufs=B))
-        pairs = ctx.enter_context(tc.tile_pool(name="pairs", bufs=N_PAIRS))
         psum = ctx.enter_context(tc.psum_pool(name="psum", bufs=8))
 
         zeros = keep.tile([P, BANK], BF16)
@@ -46,7 +45,7 @@ def tile_sparseconv2d_kernel(tc, inputs, kernel_words, kernel_scales, out):
             nc.tensor.matmul(out=unread[:], lhsT=zeros[:, :P], rhs=zeros[:], start=True, stop=True)
 
         w_scales = keep.tile([P, TAPS * TAPS, F], U8, align_bytes=64)
-        x_scales = keep.tile([P, N_PAIRS, H * ROW], U8, align_bytes=64)
+        x_scales = keep.tile([P, B * PLANE], U8, align_bytes=64)
         nc.vector.memset(w_scales[:].bitcast(I32), 0)
         nc.vector.memset(x_scales[:].bitcast(I32), 0)
 
@@ -65,127 +64,159 @@ def tile_sparseconv2d_kernel(tc, inputs, kernel_words, kernel_scales, out):
             taps = slice(TAPS * i, TAPS * (i + 1))
             nc.sync.dma_start(out=w_words[:, taps, :].bitcast(I32), in_=words[:, taps, :])
 
-        x_raws = [load_image(b) for b in range(PAIR)]
+        x_raws = [load_image(0)]
         scale_rows = kernel_scales.rearrange("g (q r) n -> r q g n", r=4)
         for r in range(4):
             nc.sync.dma_start(out=w_scales[r:P:32, :, :].bitcast(I32), in_=scale_rows[r].bitcast(I32))
-        load_weights(0)
-        load_weights(1)
-        x_raws.extend(load_image(b) for b in range(PAIR, 2 * PAIR))
-        load_weights(2)
-        x_raws.extend(load_image(b) for b in range(2 * PAIR, B))
+        for i in range(TAPS):
+            x_raws.append(load_image(1 + i))
+            load_weights(i)
+        x_raws.extend(load_image(b) for b in range(1 + TAPS, B))
 
-        def regroup(g, vector_rows):
-            grouped = pairs.tile([P, H * PAIR * W * PACK], BF16, align_bytes=64, name="grouped")
-            order = "p (s h w t) -> p h s w t" if g == N_PAIRS - 1 else "p (h s w t) -> p h s w t"
-            places = grouped[:].rearrange(order, s=PAIR, w=W, t=PACK)
-            for s in range(PAIR):
-                pixels = x_raws[PAIR * g + s][:].rearrange("p t (h w) -> p h w t", w=W)
-                nc.vector.tensor_copy(out=places[:, :vector_rows, s, :, :], in_=pixels[:, :vector_rows])
-                nc.scalar.copy(out=places[:, vector_rows:, s, :, :], in_=pixels[:, vector_rows:])
-            return grouped
+        grouped = {}
+        codes = {}
+        windows = {}
 
-        def quantise(g, grouped):
-            codes = pairs.tile([P, H * ROW], U32, align_bytes=64, name="codes")
+        def regroup(b):
+            if b == JOINT[0] or b not in JOINT:
+                n = PAIR if b in JOINT else 1
+                grouped[b] = images.tile([P, n * IMAGE * PACK], BF16, align_bytes=64, name="grouped_%d" % n)
+            else:
+                grouped[b] = grouped[JOINT[0]]
+            if b in JOINT:
+                places = grouped[b][:].rearrange("p (h s w t) -> p h s w t", s=PAIR, w=W, t=PACK)[:, :, b - JOINT[0]]
+            else:
+                places = grouped[b][:].rearrange("p (h w t) -> p h w t", w=W, t=PACK)
+            pixels = x_raws[b][:].rearrange("p t (h w) -> p h w t", w=W)
+            cut = VECTOR_ROWS[b]
+            nc.vector.tensor_copy(out=places[:, :cut], in_=pixels[:, :cut])
+            nc.scalar.copy(out=places[:, cut:], in_=pixels[:, cut:])
+
+        def quantise(b, n=1):
+            codes[b] = images.tile([P, n * IMAGE], U32, align_bytes=64, name="codes_%d" % n)
             for h0, h1 in ((0, OUT_D), (OUT_D, H)):
+                cols = slice(h0 * n * W, h1 * n * W)
                 nc.vector.quantize_mx(
-                    out=codes[:, h0 * ROW : h1 * ROW].bitcast(FP8X4),
-                    scales=x_scales[:, g, h0 * ROW : h1 * ROW],
-                    in_=grouped[:, h0 * ROW * PACK : h1 * ROW * PACK],
+                    out=codes[b][:, cols].bitcast(FP8X4),
+                    scales=x_scales[:, b * PLANE :][:, cols],
+                    in_=grouped[b][:, h0 * n * W * PACK : h1 * n * W * PACK],
                 )
-            return codes
 
-        def shift_scales(g):
-            from_row_1 = pairs.tile([P, BANK], U8, align_bytes=64, name="from_row_1")
-            nc.vector.tensor_copy(out=from_row_1[:].bitcast(I32), in_=x_scales[:, g, ROW : ROW + BANK].bitcast(I32))
-            return [x_scales[:, g, 0:BANK], from_row_1[:], x_scales[:, g, 2 * ROW : 2 * ROW + BANK]]
+        def shift_scales(b, n=1):
+            width = n * HALF
+            plane = x_scales[:, b * PLANE : b * PLANE + n * IMAGE]
+            windows[b] = {0: plane[:, :width]}
+            for j in (2, 1):
+                first = j * n * W
+                if first % 64 == 0:
+                    windows[b][j] = plane[:, first : first + width]
+                else:
+                    moved = images.tile([P, width], U8, align_bytes=64, name="moved_%d_%d" % (n, j))
+                    nc.vector.tensor_copy(out=moved[:].bitcast(I32), in_=plane[:, first : first + width].bitcast(I32))
+                    windows[b][j] = moved[:]
 
-        def multiply(i, codes, window_scales):
-            partial = psum.tile([P, BANK], F32, name="partial")
+        def multiply(partial, i, b, n=1, d0=0, d1=OUT_D):
+            row = n * W
             for j in ROW_TAPS:
                 nc.tensor.matmul_mx(
-                    out=partial[:],
+                    out=partial,
                     lhsT=w_words[:, TAPS * i + j, :].bitcast(FP8X4),
                     lhsT_scale=w_scales[:, TAPS * i + j, :],
-                    rhs=codes[:, j * ROW : j * ROW + BANK].bitcast(FP8X4),
-                    rhs_scale=window_scales[j],
+                    rhs=codes[b][:, (j + d0) * row : (j + d1) * row].bitcast(FP8X4),
+                    rhs_scale=windows[b][j][:, d0 * row : d1 * row],
                     start=(j == ROW_TAPS[0]),
                     stop=(j == ROW_TAPS[-1]),
                 )
-            return partial[:].rearrange("p (d s w) -> p s w d", s=PAIR, w=W)[:, :, i : i + OUT_A, :]
 
-        def shift_scales_of_images(g):
-            moved = pairs.tile([P, TAPS, BANK], U8, align_bytes=64, name="moved")
-            windows = {(0, 0): x_scales[:, g, 0:HALF], (1, 2): x_scales[:, g, IMAGE + 2 * W : IMAGE + 2 * W + HALF]}
-            for k, (first, images_served) in enumerate(((2 * W, ((0, 2), (1, 0))), (W, ((0, 1),)), (IMAGE + W, ((1, 1),)))):
-                width = HALF * len(images_served)
-                nc.vector.tensor_copy(
-                    out=moved[:, k, :width].bitcast(I32), in_=x_scales[:, g, first : first + width].bitcast(I32)
-                )
-                for n, key in enumerate(images_served):
-                    windows[key] = moved[:, k, n * HALF : (n + 1) * HALF]
-            return windows
+        def banks_of_pair():
+            return [psum.tile([P, BANK], F32, name="partial") for i in range(TAPS)]
 
-        def multiply_image(i, s, codes, windows, d0=0, d1=OUT_D):
-            partial = psum.tile([P, (d1 - d0) * W], F32, name="partial")
-            for j in ROW_TAPS:
-                first = IMAGE * s + W * j
-                nc.tensor.matmul_mx(
-                    out=partial[:],
-                    lhsT=w_words[:, TAPS * i + j, :].bitcast(FP8X4),
-                    lhsT_scale=w_scales[:, TAPS * i + j, :],
-                    rhs=codes[:, first + d0 * W : first + d1 * W].bitcast(FP8X4),
-                    rhs_scale=windows[(s, j)][:, d0 * W : d1 * W],
-                    start=(j == ROW_TAPS[0]),
-                    stop=(j == ROW_TAPS[-1]),
-                )
-            return partial[:].rearrange("p (d w) -> p w d", w=W)[:, i : i + OUT_A, :]
+        def by_image(bank, i):
+            return bank[:].rearrange("p (s d w) -> p s w d", s=PAIR, w=W)[:, :, i : i + OUT_A, :]
+
+        def by_row(bank, i):
+            return bank[:].rearrange("p (d s w) -> p s w d", s=PAIR, w=W)[:, :, i : i + OUT_A, :]
+
+        def new_result():
+            return images.tile([P, PAIR, OUT_A, OUT_D], F32, name="result")
+
+        def store_pair(b, result):
+            nc.sync.dma_start(
+                out=out[b : b + PAIR].rearrange("s f a d -> f s (a d)"), in_=result[:].rearrange("p s a d -> p s (a d)")
+            )
 
         with tc.manual_schedule():
-            operands = []
-            for step in range(N_PAIRS + AHEAD):
-                feeds = step < N_PAIRS
-                g = step - AHEAD
-                sums = 0 <= g < N_PAIRS - 1
-                if g == N_PAIRS - 1:
-                    codes, window_scales = operands[g]
-                    results = []
-                    for s in range(PAIR):
-                        shifted = [multiply_image(i, s, codes, window_scales) for i in range(TAPS - 1)]
-                        result = pairs.tile([P, OUT_A, OUT_D], F32, name="result_of_image")
-                        nc.scalar.copy(out=result[:], in_=shifted[0])
-                        nc.vector.tensor_add(out=result[:], in0=shifted[1], in1=result[:])
-                        results.append(result)
-                    for s in range(PAIR):
-                        result = results[s]
-                        for d0, d1 in ((0, OUT_D),) if s == 0 else ((0, OUT_D // 2), (OUT_D // 2, OUT_D)):
-                            nc.vector.tensor_add(
-                                out=result[:, :, d0:d1],
-                                in0=multiply_image(TAPS - 1, s, codes, window_scales, d0, d1),
-                                in1=result[:, :, d0:d1],
-                            )
-                        nc.sync.dma_start(
-                            out=out[PAIR * g + s].rearrange("f a d -> f (a d)"), in_=result[:].rearrange("p a d -> p (a d)")
-                        )
-                if sums:
-                    codes, window_scales = operands[g]
-                    shifted = [multiply(i, codes, window_scales) for i in range(TAPS)]
-                    result = pairs.tile([P, PAIR, OUT_A, OUT_D], F32, name="result")
-                    nc.scalar.copy(out=result[:], in_=shifted[0])
-                if feeds:
-                    grouped = regroup(step, VECTOR_ROWS_BESIDE_SUMS if sums else VECTOR_ROWS_AT_FIRST)
-                if sums:
-                    nc.vector.tensor_add(out=result[:], in0=shifted[1], in1=result[:])
-                if feeds:
-                    new_codes = quantise(step, grouped)
-                if sums:
-                    nc.vector.tensor_add(out=result[:], in0=shifted[2], in1=result[:])
-                if feeds:
-                    operands.append(
-                        (new_codes, shift_scales_of_images(step) if step == N_PAIRS - 1 else shift_scales(step))
+            first = banks_of_pair()
+            second = banks_of_pair()
+
+            def half(b, i):
+                return (first if b < PAIR else second)[i][:, (b % PAIR) * HALF : (b % PAIR + 1) * HALF]
+
+            regroup(0)
+            quantise(0)
+            regroup(1)
+            shift_scales(0)
+            quantise(1)
+            regroup(2)
+            shift_scales(1)
+            for i in range(TAPS):
+                for b in range(PAIR):
+                    multiply(half(b, i), i, b)
+            result_a = new_result()
+            nc.scalar.copy(out=result_a[:], in_=by_image(first[0], 0))
+            quantise(2)
+            regroup(3)
+            shift_scales(2)
+            quantise(3)
+            regroup(4)
+            shift_scales(3)
+            for b in (2, 3):
+                for i in range(TAPS):
+                    multiply(half(b, i), i, b)
+            regroup(5)
+            nc.vector.tensor_add(out=result_a[:], in0=by_image(first[1], 1), in1=result_a[:])
+            quantise(4, PAIR)
+            regroup(6)
+            shift_scales(4, PAIR)
+            nc.vector.tensor_add(out=result_a[:], in0=by_image(first[2], 2), in1=result_a[:])
+            store_pair(0, result_a)
+            third = banks_of_pair()
+            for i in range(TAPS):
+                multiply(third[i][:], i, 4, PAIR)
+            quantise(6)
+            result_b = new_result()
+            nc.scalar.copy(out=result_b[:], in_=by_image(second[0], 0))
+            regroup(7)
+            shift_scales(6)
+            quantise(7)
+            nc.vector.tensor_add(out=result_b[:], in0=by_image(second[1], 1), in1=result_b[:])
+            shift_scales(7)
+            nc.vector.tensor_add(out=result_b[:], in0=by_image(second[2], 2), in1=result_b[:])
+            store_pair(2, result_b)
+            result_c = new_result()
+            nc.scalar.copy(out=result_c[:], in_=by_row(third[0], 0))
+            nc.vector.tensor_add(out=result_c[:], in0=by_row(third[1], 1), in1=result_c[:])
+            nc.vector.tensor_add(out=result_c[:], in0=by_row(third[2], 2), in1=result_c[:])
+            store_pair(4, result_c)
+
+            def one_image(i, b, d0=0, d1=OUT_D):
+                partial = psum.tile([P, (d1 - d0) * W], F32, name="partial")
+                multiply(partial[:], i, b, 1, d0, d1)
+                return partial[:].rearrange("p (d w) -> p w d", w=W)[:, i : i + OUT_A, :]
+
+            results = {}
+            for b in (6, 7):
+                shifted = [one_image(i, b) for i in range(2)]
+                result = images.tile([P, OUT_A, OUT_D], F32, name="result_of_image")
+                nc.scalar.copy(out=result[:], in_=shifted[0])
+                nc.vector.tensor_add(out=result[:], in0=shifted[1], in1=result[:])
+                results[b] = result
+            for b in (6, 7):
+                result = results[b]
+                for d0, d1 in ((0, OUT_D),) if b == 6 else ((0, OUT_D // 2), (OUT_D // 2, OUT_D)):
+                    nc.vector.tensor_add(
+                        out=result[:, :, d0:d1], in0=one_image(2, b, d0, d1), in1=result[:, :, d0:d1]
                     )
-                if sums:
-                    nc.sync.dma_start(
-                        out=out[PAIR * g : PAIR * (g + 1)].rearrange("s f a d -> f s (a d)"),
-                        in_=result[:].rearrange("p s a d -> p s (a d)"),
-                    )
+                nc.sync.dma_start(
+                    out=out[b].rearrange("f a d -> f (a d)"), in_=result[:].rearrange("p a d -> p (a d)")
+                )

@@ -26,7 +26,7 @@ PLANE = 320
 SINGLES = (0, 1, 2, 3, 6, 7)
 JOINT = (4, 5)
 WARM_UP = 6
-VECTOR_ROWS = (12, 12, 10, 10, 8, 8, 6, 6)
+VECTOR_ROWS = (12, 12, 10, 10, 10, 10, 2, 2)
 
 FLOPS = 2 * B * OUT_A * OUT_D * TAPS * TAPS * C * F
 
@@ -68,10 +68,12 @@ def tile_sparseconv2d_kernel(tc, inputs, kernel_words, kernel_scales, out):
         scale_rows = kernel_scales.rearrange("g (q r) n -> r q g n", r=4)
         for r in range(4):
             nc.sync.dma_start(out=w_scales[r:P:32, :, :].bitcast(I32), in_=scale_rows[r].bitcast(I32))
-        for i in range(TAPS):
-            x_raws.append(load_image(1 + i))
-            load_weights(i)
-        x_raws.extend(load_image(b) for b in range(1 + TAPS, B))
+        x_raws.append(load_image(1))
+        load_weights(0)
+        load_weights(1)
+        x_raws.append(load_image(2))
+        load_weights(2)
+        x_raws.extend(load_image(b) for b in range(3, B))
 
         grouped = {}
         codes = {}
@@ -157,15 +159,17 @@ def tile_sparseconv2d_kernel(tc, inputs, kernel_words, kernel_scales, out):
             regroup(1)
             shift_scales(0)
             quantise(1)
-            regroup(2)
             shift_scales(1)
-            for i in range(TAPS):
-                for b in range(PAIR):
+            regroup(2)
+            for b in range(PAIR):
+                for i in range(TAPS - 1):
                     multiply(half(b, i), i, b)
-            result_a = new_result()
-            nc.scalar.copy(out=result_a[:], in_=by_image(first[0], 0))
+            for b in range(PAIR):
+                multiply(half(b, TAPS - 1), TAPS - 1, b)
             quantise(2)
             regroup(3)
+            result_a = new_result()
+            nc.scalar.copy(out=result_a[:], in_=by_image(first[0], 0))
             shift_scales(2)
             quantise(3)
             regroup(4)
@@ -177,22 +181,22 @@ def tile_sparseconv2d_kernel(tc, inputs, kernel_words, kernel_scales, out):
             nc.vector.tensor_add(out=result_a[:], in0=by_image(first[1], 1), in1=result_a[:])
             quantise(4, PAIR)
             regroup(6)
+            result_b = new_result()
+            nc.scalar.copy(out=result_b[:], in_=by_image(second[0], 0))
             shift_scales(4, PAIR)
+            regroup(7)
             nc.vector.tensor_add(out=result_a[:], in0=by_image(first[2], 2), in1=result_a[:])
             store_pair(0, result_a)
             third = banks_of_pair()
             for i in range(TAPS):
                 multiply(third[i][:], i, 4, PAIR)
             quantise(6)
-            result_b = new_result()
-            nc.scalar.copy(out=result_b[:], in_=by_image(second[0], 0))
-            regroup(7)
+            nc.vector.tensor_add(out=result_b[:], in0=by_image(second[1], 1), in1=result_b[:])
             shift_scales(6)
             quantise(7)
-            nc.vector.tensor_add(out=result_b[:], in0=by_image(second[1], 1), in1=result_b[:])
-            shift_scales(7)
             nc.vector.tensor_add(out=result_b[:], in0=by_image(second[2], 2), in1=result_b[:])
             store_pair(2, result_b)
+            shift_scales(7)
             result_c = new_result()
             nc.scalar.copy(out=result_c[:], in_=by_row(third[0], 0))
             nc.vector.tensor_add(out=result_c[:], in0=by_row(third[1], 1), in1=result_c[:])

@@ -26,7 +26,7 @@ PLANE = 320
 SINGLES = (0, 1, 2, 3, 6, 7)
 JOINT = (4, 5)
 WARM_UP = 6
-VECTOR_ROWS = (12, 12, 10, 10, 10, 10, 2, 2)
+VECTOR_ROWS = (12, 12, 12, 12, 10, 10, 2, 2)
 
 FLOPS = 2 * B * OUT_A * OUT_D * TAPS * TAPS * C * F
 
@@ -94,9 +94,9 @@ def tile_sparseconv2d_kernel(tc, inputs, kernel_words, kernel_scales, out):
             nc.vector.tensor_copy(out=places[:, :cut], in_=pixels[:, :cut])
             nc.scalar.copy(out=places[:, cut:], in_=pixels[:, cut:])
 
-        def quantise(b, n=1):
+        def quantise(b, n=1, last_rows_first=False):
             codes[b] = images.tile([P, n * IMAGE], U32, align_bytes=64, name="codes_%d" % n)
-            for h0, h1 in ((0, OUT_D), (OUT_D, H)):
+            for h0, h1 in ((OUT_D, H), (0, OUT_D)) if last_rows_first else ((0, OUT_D), (OUT_D, H)):
                 cols = slice(h0 * n * W, h1 * n * W)
                 nc.vector.quantize_mx(
                     out=codes[b][:, cols].bitcast(FP8X4),
@@ -117,9 +117,9 @@ def tile_sparseconv2d_kernel(tc, inputs, kernel_words, kernel_scales, out):
                     nc.vector.tensor_copy(out=moved[:].bitcast(I32), in_=plane[:, first : first + width].bitcast(I32))
                     windows[b][j] = moved[:]
 
-        def multiply(partial, i, b, n=1, d0=0, d1=OUT_D):
+        def multiply(partial, i, b, n=1, d0=0, d1=OUT_D, row_taps=ROW_TAPS):
             row = n * W
-            for j in ROW_TAPS:
+            for j in row_taps:
                 nc.tensor.matmul_mx(
                     out=partial,
                     lhsT=w_words[:, TAPS * i + j, :].bitcast(FP8X4),
@@ -155,18 +155,20 @@ def tile_sparseconv2d_kernel(tc, inputs, kernel_words, kernel_scales, out):
                 return (first if b < PAIR else second)[i][:, (b % PAIR) * HALF : (b % PAIR + 1) * HALF]
 
             regroup(0)
-            quantise(0)
+            quantise(0, last_rows_first=True)
             regroup(1)
             shift_scales(0)
             quantise(1)
             shift_scales(1)
             regroup(2)
-            for b in range(PAIR):
+            for i in range(TAPS - 1):
+                multiply(half(0, i), i, 0)
+            for row_taps in (ROW_TAPS[:1], ROW_TAPS[1:]):
                 for i in range(TAPS - 1):
-                    multiply(half(b, i), i, b)
+                    multiply(half(1, i), i, 1, row_taps=row_taps)
             for b in range(PAIR):
                 multiply(half(b, TAPS - 1), TAPS - 1, b)
-            quantise(2)
+            quantise(2, last_rows_first=True)
             regroup(3)
             result_a = new_result()
             nc.scalar.copy(out=result_a[:], in_=by_image(first[0], 0))
@@ -175,8 +177,10 @@ def tile_sparseconv2d_kernel(tc, inputs, kernel_words, kernel_scales, out):
             regroup(4)
             shift_scales(3)
             for b in (2, 3):
-                for i in range(TAPS):
-                    multiply(half(b, i), i, b)
+                for row_taps in (ROW_TAPS[:1], ROW_TAPS[1:]):
+                    for i in range(TAPS - 1):
+                        multiply(half(b, i), i, b, row_taps=row_taps)
+                multiply(half(b, TAPS - 1), TAPS - 1, b)
             regroup(5)
             nc.vector.tensor_add(out=result_a[:], in0=by_image(first[1], 1), in1=result_a[:])
             quantise(4, PAIR)

from contextlib import ExitStack

import concourse.mybir as mybir

BF16 = mybir.dt.bfloat16
F32 = mybir.dt.float32
I32 = mybir.dt.int32
U8 = mybir.dt.uint8
U32 = mybir.dt.uint32
FP8X4 = mybir.dt.float8_e4m3fn_x4

P = 128
PACK = 4
B, C, H, W, F = 8, 512, 18, 16, 128
TAPS = 3
ROW_TAPS = (0, 2, 1)
OUT_D = H - TAPS + 1
OUT_A = W - TAPS + 1

PAIR = 2
ROW = PAIR * W
BANK = OUT_D * ROW
IMAGE = H * W
HALF = OUT_D * W
PLANE = 320
SINGLES = (0, 1, 2, 3, 6, 7)
JOINT = (4, 5)
WARM_UP = 6
VECTOR_ROWS = (12, 12, 12, 12, 10, 10, 2, 2)

FLOPS = 2 * B * OUT_A * OUT_D * TAPS * TAPS * C * F


def tile_sparseconv2d_kernel(tc, inputs, kernel_words, kernel_scales, out):
    nc = tc.nc
    with ExitStack() as ctx:
        keep = ctx.enter_context(tc.tile_pool(name="keep", bufs=1))
        images = ctx.enter_context(tc.tile_pool(name="images", bufs=B))
        psum = ctx.enter_context(tc.psum_pool(name="psum", bufs=8))

        zeros = keep.tile([P, BANK], BF16)
        nc.vector.memset(zeros[:], 0.0)
        unread = psum.tile([P, BANK], F32, name="partial")
        for warm in range(WARM_UP):
            nc.tensor.matmul(out=unread[:], lhsT=zeros[:, :P], rhs=zeros[:], start=True, stop=True)

        w_scales = keep.tile([P, TAPS * TAPS, F], U8, align_bytes=64)
        x_scales = keep.tile([P, B * PLANE], U8, align_bytes=64)
        nc.vector.memset(w_scales[:].bitcast(I32), 0)
        nc.vector.memset(x_scales[:].bitcast(I32), 0)

        def load_image(b):
            x_raw = images.tile([P, PACK, H * W], BF16, name="x_raw")
            nc.sync.dma_start(
                out=x_raw[:].rearrange("p t n -> p (t n)"),
                in_=inputs[b].rearrange("(p t) h w -> p (t h w)", t=PACK),
            )
            return x_raw

        w_words = keep.tile([P, TAPS * TAPS, F], U32, align_bytes=64)
        words = kernel_words.rearrange("g p n t -> p g (n t)").bitcast(I32)

        def load_weights(i):
            taps = slice(TAPS * i, TAPS * (i + 1))
            nc.sync.dma_start(out=w_words[:, taps, :].bitcast(I32), in_=words[:, taps, :])

        x_raws = [load_image(0)]
        scale_rows = kernel_scales.rearrange("g (q r) n -> r q g n", r=4)
        for r in range(4):
            nc.sync.dma_start(out=w_scales[r:P:32, :, :].bitcast(I32), in_=scale_rows[r].bitcast(I32))
        x_raws.append(load_image(1))
        load_weights(0)
        load_weights(1)
        x_raws.append(load_image(2))
        load_weights(2)
        x_raws.extend(load_image(b) for b in range(3, B))

        grouped = {}
        codes = {}
        windows = {}

        def regroup(b):
            if b == JOINT[0] or b not in JOINT:
                n = PAIR if b in JOINT else 1
                grouped[b] = images.tile([P, n * IMAGE * PACK], BF16, align_bytes=64, name="grouped_%d" % n)
            else:
                grouped[b] = grouped[JOINT[0]]
            if b in JOINT:
                places = grouped[b][:].rearrange("p (h s w t) -> p h s w t", s=PAIR, w=W, t=PACK)[:, :, b - JOINT[0]]
            else:
                places = grouped[b][:].rearrange("p (h w t) -> p h w t", w=W, t=PACK)
            pixels = x_raws[b][:].rearrange("p t (h w) -> p h w t", w=W)
            cut = VECTOR_ROWS[b]
            nc.vector.tensor_copy(out=places[:, :cut], in_=pixels[:, :cut])
            nc.scalar.copy(out=places[:, cut:], in_=pixels[:, cut:])

        def quantise(b, n=1, last_rows_first=False):
            codes[b] = images.tile([P, n * IMAGE], U32, align_bytes=64, name="codes_%d" % n)
            for h0, h1 in ((OUT_D, H), (0, OUT_D)) if last_rows_first else ((0, OUT_D), (OUT_D, H)):
                cols = slice(h0 * n * W, h1 * n * W)
                nc.vector.quantize_mx(
                    out=codes[b][:, cols].bitcast(FP8X4),
                    scales=x_scales[:, b * PLANE :][:, cols],
                    in_=grouped[b][:, h0 * n * W * PACK : h1 * n * W * PACK],
                )

        def shift_scales(b, n=1):
            width = n * HALF
            plane = x_scales[:, b * PLANE : b * PLANE + n * IMAGE]
            windows[b] = {0: plane[:, :width]}
            for j in (2, 1):
                first = j * n * W
                if first % 64 == 0:
                    windows[b][j] = plane[:, first : first + width]
                else:
                    moved = images.tile([P, width], U8, align_bytes=64, name="moved_%d_%d" % (n, j))
                    nc.vector.tensor_copy(out=moved[:].bitcast(I32), in_=plane[:, first : first + width].bitcast(I32))
                    windows[b][j] = moved[:]

        def multiply(partial, i, b, n=1, d0=0, d1=OUT_D, row_taps=ROW_TAPS):
            row = n * W
            for j in row_taps:
                nc.tensor.matmul_mx(
                    out=partial,
                    lhsT=w_words[:, TAPS * i + j, :].bitcast(FP8X4),
                    lhsT_scale=w_scales[:, TAPS * i + j, :],
                    rhs=codes[b][:, (j + d0) * row : (j + d1) * row].bitcast(FP8X4),
                    rhs_scale=windows[b][j][:, d0 * row : d1 * row],
                    start=(j == ROW_TAPS[0]),
                    stop=(j == ROW_TAPS[-1]),
                )

        def banks_of_pair():
            return [psum.tile([P, BANK], F32, name="partial") for i in range(TAPS)]

        def by_image(bank, i):
            return bank[:].rearrange("p (s d w) -> p s w d", s=PAIR, w=W)[:, :, i : i + OUT_A, :]

        def by_row(bank, i):
            return bank[:].rearrange("p (d s w) -> p s w d", s=PAIR, w=W)[:, :, i : i + OUT_A, :]

        def new_result():
            return images.tile([P, PAIR, OUT_A, OUT_D], F32, name="result")

        def store_pair(b, result):
            nc.sync.dma_start(
                out=out[b : b + PAIR].rearrange("s f a d -> f s (a d)"), in_=result[:].rearrange("p s a d -> p s (a d)")
            )

        with tc.manual_schedule():
            first = banks_of_pair()
            second = banks_of_pair()

            def half(b, i):
                return (first if b < PAIR else second)[i][:, (b % PAIR) * HALF : (b % PAIR + 1) * HALF]

            regroup(0)
            quantise(0, last_rows_first=True)
            regroup(1)
            shift_scales(0)
            quantise(1)
            shift_scales(1)
            regroup(2)
            for i in range(TAPS - 1):
                multiply(half(0, i), i, 0)
            for row_taps in (ROW_TAPS[:1], ROW_TAPS[1:]):
                for i in range(TAPS - 1):
                    multiply(half(1, i), i, 1, row_taps=row_taps)
            for b in range(PAIR):
                multiply(half(b, TAPS - 1), TAPS - 1, b)
            quantise(2, last_rows_first=True)
            regroup(3)
            result_a = new_result()
            nc.scalar.copy(out=result_a[:], in_=by_image(first[0], 0))
            shift_scales(2)
            quantise(3)
            regroup(4)
            shift_scales(3)
            for b in (2, 3):
                for row_taps in (ROW_TAPS[:1], ROW_TAPS[1:]):
                    for i in range(TAPS - 1):
                        multiply(half(b, i), i, b, row_taps=row_taps)
                multiply(half(b, TAPS - 1), TAPS - 1, b)
            regroup(5)
            nc.vector.tensor_add(out=result_a[:], in0=by_image(first[1], 1), in1=result_a[:])
            quantise(4, PAIR)
            regroup(6)
            result_b = new_result()
            nc.scalar.copy(out=result_b[:], in_=by_image(second[0], 0))
            shift_scales(4, PAIR)
            regroup(7)
            nc.vector.tensor_add(out=result_a[:], in0=by_image(first[2], 2), in1=result_a[:])
            store_pair(0, result_a)
            third = banks_of_pair()
            for i in range(TAPS):
                multiply(third[i][:], i, 4, PAIR)
            quantise(6)
            nc.vector.tensor_add(out=result_b[:], in0=by_image(second[1], 1), in1=result_b[:])
            shift_scales(6)
            quantise(7)
            nc.vector.tensor_add(out=result_b[:], in0=by_image(second[2], 2), in1=result_b[:])
            store_pair(2, result_b)
            shift_scales(7)
            result_c = new_result()
            nc.scalar.copy(out=result_c[:], in_=by_row(third[0], 0))
            nc.vector.tensor_add(out=result_c[:], in0=by_row(third[1], 1), in1=result_c[:])
            nc.vector.tensor_add(out=result_c[:], in0=by_row(third[2], 2), in1=result_c[:])
            store_pair(4, result_c)

            def one_image(i, b, d0=0, d1=OUT_D):
                partial = psum.tile([P, (d1 - d0) * W], F32, name="partial")
                multiply(partial[:], i, b, 1, d0, d1)
                return partial[:].rearrange("p (d w) -> p w d", w=W)[:, i : i + OUT_A, :]

            results = {}
            for b in (6, 7):
                shifted = [one_image(i, b) for i in range(2)]
                result = images.tile([P, OUT_A, OUT_D], F32, name="result_of_image")
                nc.scalar.copy(out=result[:], in_=shifted[0])
                nc.vector.tensor_add(out=result[:], in0=shifted[1], in1=result[:])
                results[b] = result
            for b in (6, 7):
                result = results[b]
                for d0, d1 in ((0, OUT_D),) if b == 6 else ((0, OUT_D // 2), (OUT_D // 2, OUT_D)):
                    nc.vector.tensor_add(
                        out=result[:, :, d0:d1], in0=one_image(2, b, d0, d1), in1=result[:, :, d0:d1]
                    )
                nc.sync.dma_start(
                    out=out[b].rearrange("f a d -> f (a d)"), in_=result[:].rearrange("p a d -> p (a d)")
                )
